import numpy as np
import ml_dtypes


def mxq(x, axis, fmt="e4m3"):
    dtype, down = {"e4m3": (ml_dtypes.float8_e4m3fn, 7), "e5m2": (ml_dtypes.float8_e5m2, 14)}[fmt]
    v = np.moveaxis(np.asarray(x, np.float32).astype(ml_dtypes.bfloat16).astype(np.float64), axis, -1)
    blocks = v.reshape(v.shape[:-1] + (-1, 32))
    amax = np.abs(blocks).max(-1, keepdims=True)
    byte = np.maximum(np.where(amax > 0, np.frexp(amax)[1] - 1 + 127, 0) - down, 1)
    scale = np.exp2(byte - 127.0)
    codes = (blocks / scale).astype(np.float32).astype(dtype).astype(np.float64)
    return np.moveaxis((codes * scale).reshape(v.shape), -1, axis)


WIDE = False


def mx_kscale(k):
    if not WIDE:
        return np.ones(k)
    levels = np.array([10, -10, 5, -5, 0])
    if k % 512:
        return np.exp2(np.random.permutation(np.resize(levels, k // 32))).repeat(32)
    a = np.empty((k // 512, 16))
    for p in range(k // 512):
        a[p, :8] = np.random.permutation(np.resize(levels, 8))
        for g in range(8):
            far = levels[np.abs(levels - a[p, g]) >= 10]
            a[p, g + 8] = far[np.random.randint(len(far))]
    return np.exp2(a.ravel()).repeat(32)


BF16 = ml_dtypes.bfloat16


def bf(x):
    return np.asarray(x, np.float32).astype(BF16)


def f64(x):
    return np.asarray(x).astype(np.float64)


B, N, M, D = 4, 1024, 1024, 512


def sigmoid(x):
    return 1.0 / (1.0 + np.exp(-x))


def setup_inputs():
    s = mx_kscale(M)
    wq = np.random.standard_normal((D, D + 1)) / np.sqrt(D)
    wq[:, D] *= np.sqrt(D)
    return {"encoded_last_node": bf(np.random.standard_normal((B, N, D))),
            "load": bf(np.random.random((B, N))),
            "cur_dist": bf(np.random.random((B, N, M))),
            "log_scale": bf(2.0 + 0.1 * np.random.standard_normal(1)),
            "ninf_mask": bf(np.where(np.random.random((B, N, M)) < 0.25, -6.0, 0.0) + np.log(s)),
            "k": bf(np.random.standard_normal((B, M, D)) - np.log(s)[:, None]),
            "v": bf(np.random.standard_normal((B, M, D)) * 3.0),
            "Wq_last": bf(wq),
            "alpha1": bf(1.5 + 0.1 * np.random.standard_normal(1))}


def reference(encoded_last_node, load, cur_dist, log_scale, ninf_mask, k, v, Wq_last, alpha1):
    wq = f64(Wq_last)
    q = f64(encoded_last_node) @ wq[:, :D].T + f64(load)[:, :, None] * wq[:, D]
    eb = np.exp(-f64(alpha1)[0] * f64(log_scale)[0] * f64(cur_dist) + f64(ninf_mask))
    ek = np.exp(f64(k))
    ebq = mxq(eb, 2, "e4m3")
    num = ebq @ mxq(ek * f64(v), 1, "e4m3")
    den = ebq @ mxq(ek, 1, "e4m3")
    return sigmoid(q) * (num / den)

@@ -1,0 +1,367 @@
+from contextlib import ExitStack
+
+import concourse.mybir as mybir
+from concourse.masks import make_identity
+
+F32 = mybir.dt.float32
+BF16 = mybir.dt.bfloat16
+U32 = mybir.dt.uint32
+U8 = mybir.dt.uint8
+FP8X4 = mybir.dt.float8_e4m3fn_x4
+ACT = mybir.ActivationFunctionType
+ALU = mybir.AluOpType
+
+B, N, M, D = 4, 1024, 1024, 512
+FLOPS = 2 * B * N * D * (D + 1) + 2 * 2 * B * N * M * D
+
+P = 128
+PACK = 4
+K_PASS = P * PACK
+PASSES = M // K_PASS
+TILES_PER_BATCH = N // P
+TILES = B * TILES_PER_BATCH
+LOAD_TILES = TILES_PER_BATCH // 2
+F_CHUNKS = D // P
+T_PER_MATMUL = (M // P + F_CHUNKS) // F_CHUNKS
+PIECE = P
+PIECES_PER_PASS = D // PIECE
+PIECES_PER_BATCH = PASSES * PIECES_PER_PASS
+PIECES = B * PIECES_PER_BATCH
+assert PIECES_PER_BATCH == TILES_PER_BATCH
+RUN = 4
+
+EXPONENT_LEAD = 3
+TRANSPOSE_LEAD = 2
+EXP_LEAD = 1
+NUM_LAG = 1
+MERGE_LAG = 2
+RECIP_LAG = TILES_PER_BATCH
+FINISH_LAG = RECIP_LAG + 1
+DMA_STEPS = 3
+LOAD_LEAD = EXPONENT_LEAD + DMA_STEPS
+KEY_LEAD = PIECES_PER_BATCH
+KEY_LOAD_LEAD = KEY_LEAD + DMA_STEPS
+FIRST_STEP = -LOAD_LEAD
+LAST_STEP = TILES - 1 + FINISH_LAG
+
+
+def tile_cvrp_decoder_pa_t_kernel(
+    tc, encoded_last_node, load, cur_dist, log_scale, ninf_mask, k, v, Wq_last, alpha1, out
+):
+    nc = tc.nc
+
+    dist_view = cur_dist.rearrange("b (p i) m -> b p i m", i=TILES_PER_BATCH)
+    mask_view = ninf_mask.rearrange("b (p i) m -> b p i m", i=TILES_PER_BATCH)
+    node_view = encoded_last_node.rearrange("b (p i) f -> b p i f", i=TILES_PER_BATCH)
+    out_view = out.rearrange("b (p i) d -> b p i d", i=TILES_PER_BATCH)
+    k_view = k.rearrange("b (g p j) d -> b g p j d", g=PASSES, j=PACK)
+    v_view = v.rearrange("b (g p j) d -> b g p j d", g=PASSES, j=PACK)
+
+    with ExitStack() as ctx:
+        ctx.enter_context(tc.manual_schedule())
+        consts = ctx.enter_context(tc.tile_pool(name="consts", bufs=1))
+        loads = ctx.enter_context(tc.tile_pool(name="loads", bufs=2))
+        values = ctx.enter_context(tc.tile_pool(name="values", bufs=2 * PASSES))
+        codes = ctx.enter_context(tc.tile_pool(name="codes", bufs=2))
+        stage = ctx.enter_context(tc.tile_pool(name="stage", bufs=3))
+        grouped = ctx.enter_context(tc.tile_pool(name="grouped", bufs=PASSES))
+        gates = ctx.enter_context(tc.tile_pool(name="gates", bufs=FINISH_LAG + 2))
+        logs = ctx.enter_context(tc.tile_pool(name="logs", bufs=TILES_PER_BATCH + 2))
+        psum_xt = ctx.enter_context(tc.psum_pool(name="psum_xt", bufs=3))
+        psum_et = ctx.enter_context(tc.psum_pool(name="psum_et", bufs=1))
+        psum_out = ctx.enter_context(tc.psum_pool(name="psum_out", bufs=4))
+
+        query_loads = {}
+        key_loads = {}
+        key_exp = {}
+        key_codes = {}
+        score_codes = {}
+        exponents = {}
+        transposed = {}
+        scores = {}
+        node_ps = {}
+        node_t = {}
+        q_ps = {}
+        num_ps = {}
+        gate = {}
+        log_den = {}
+
+        def is_tile(t):
+            return 0 <= t < TILES
+
+        def load_queries(h):
+            b, first = divmod(h * LOAD_TILES, TILES_PER_BATCH)
+            rows = slice(first, first + LOAD_TILES)
+            dist = loads.tile([P, LOAD_TILES, M], BF16, name="dist")
+            nc.sync.dma_start(out=dist[:], in_=dist_view[b, :, rows, :])
+            mask = loads.tile([P, LOAD_TILES, M], BF16, name="mask")
+            nc.sync.dma_start(out=mask[:], in_=mask_view[b, :, rows, :])
+            node = loads.tile([P, LOAD_TILES, D], BF16, name="node")
+            nc.sync.dma_start(out=node[:], in_=node_view[b, :, rows, :])
+            query_loads[h] = (dist, mask, node)
+
+        def load_keys(b, g):
+            k_rows = loads.tile([P, PACK, D], BF16, name="k_rows")
+            nc.sync.dma_start(out=k_rows[:], in_=k_view[b, g])
+            v_rows = values.tile([P, PACK, D], BF16, name="v_rows")
+            nc.sync.dma_start(out=v_rows[:], in_=v_view[b, g])
+            key_loads[(b, g)] = (k_rows, v_rows)
+
+        def exp_keys(piece):
+            b, rest = divmod(piece, PIECES_PER_BATCH)
+            g, part = divmod(rest, PIECES_PER_PASS)
+            if part == 0:
+                ek = stage.tile([P, PACK, D], F32, name="ek")
+                key_exp[(b, g)] = ek
+            cols = slice(part * PIECE, (part + 1) * PIECE)
+            nc.scalar.activation(
+                out=key_exp[(b, g)][:, :, cols], in_=key_loads[(b, g)][0][:, :, cols], func=ACT.Exp
+            )
+
+        def quantise_keys(b, kind):
+            words = codes.tile([P, PASSES, D], U32, name="%s_words" % kind, align_bytes=64)
+            scales = codes.tile([P, PASSES, D], U8, name="%s_scales" % kind, align_bytes=64)
+            key_codes[(b, kind)] = (words, scales)
+            rounded = []
+            for g in range(PASSES):
+                in_order = grouped.tile([P, D, PACK], BF16, name="%s_in_order" % kind, align_bytes=64)
+                out_runs = in_order[:].rearrange("p (a e) j -> p a j e", e=RUN)
+                ek_runs = key_exp[(b, g)][:].rearrange("p j (a e) -> p a j e", e=RUN)
+                if kind == "ekv":
+                    v_runs = key_loads[(b, g)][1][:].rearrange("p j (a e) -> p a j e", e=RUN)
+                    nc.vector.tensor_tensor(out=out_runs, in0=ek_runs, in1=v_runs, op=ALU.mult)
+                elif b == 0:
+                    nc.scalar.copy(out=out_runs, in_=ek_runs)
+                else:
+                    nc.vector.tensor_copy(out=out_runs, in_=ek_runs)
+                rounded.append(in_order)
+            for g in range(PASSES):
+                nc.vector.quantize_mx(
+                    out=words[:, g, :].bitcast(FP8X4),
+                    scales=scales[:, g, :],
+                    in_=rounded[g][:].rearrange("p d j -> p (d j)"),
+                )
+
+        def form_exponents(t):
+            dist, mask = query_loads[t // LOAD_TILES][0:2]
+            row = t % LOAD_TILES
+            exponent = stage.tile([P, PACK, M // PACK], F32, name="exponent")
+            nc.vector.scalar_tensor_tensor(
+                out=exponent[:],
+                in0=dist[:, row, :].rearrange("p (w j) -> p j w", j=PACK),
+                scalar=neg_slope[:, 0:1],
+                in1=mask[:, row, :].rearrange("p (w j) -> p j w", j=PACK),
+                op0=ALU.mult, op1=ALU.add,
+            )
+            exponents[t] = exponent
+
+        def transposes_for(t):
+            node = query_loads[t // LOAD_TILES][2]
+            row = t % LOAD_TILES
+            xts = []
+            for g in range(PASSES):
+                xt = psum_xt.tile([P, PACK, P], F32, name="xt")
+                xts.append(xt)
+            et = psum_et.tile([P, F_CHUNKS, P], BF16, name="et")
+            transposed[t] = xts
+            node_ps[t] = et
+
+            def exponent_block(g, j):
+                return lambda: nc.tensor.transpose(
+                    xts[g][:, j, :], exponents[t][:, j, g * P : (g + 1) * P], ident_f32[:]
+                )
+
+            def node_block(c):
+                return lambda: nc.tensor.transpose(
+                    et[:, c, :], node[:, row, c * P : (c + 1) * P], ident_bf16[:]
+                )
+
+            return (
+                [exponent_block(0, j) for j in range(PACK)]
+                + [node_block(c) for c in range(F_CHUNKS)]
+                + [exponent_block(1, j) for j in range(PACK)]
+            )
+
+        def project_and_transpose(t_q, t_next):
+            waiting = transposes_for(t_next) if is_tile(t_next) else []
+            if is_tile(t_q):
+                b, i = divmod(t_q, TILES_PER_BATCH)
+                q_acc = psum_out.tile([P, D], F32, name="q_acc", tag="out_bank")
+                q_ps[t_q] = q_acc
+            for c in range(F_CHUNKS):
+                if is_tile(t_q):
+                    nc.tensor.matmul(
+                        out=q_acc[:], lhsT=node_t[t_q][:, c, :], rhs=wq_t[:, c, :],
+                        start=(c == 0), stop=False,
+                    )
+                for transpose_block in waiting[c * T_PER_MATMUL : (c + 1) * T_PER_MATMUL]:
+                    transpose_block()
+            if is_tile(t_q):
+                nc.tensor.matmul(
+                    out=q_acc[:], lhsT=load_by_tile[:, b, i, :], rhs=wq_t[:, F_CHUNKS, :],
+                    start=False, stop=True,
+                )
+
+        def exp_scores(t):
+            eb_grouped = stage.tile([P, PASSES, P, PACK], BF16, name="eb_grouped", align_bytes=64)
+            for g in range(PASSES):
+                nc.scalar.activation(
+                    out=eb_grouped[:, g, :, :],
+                    in_=transposed[t][g][:].rearrange("p j r -> p r j"),
+                    func=ACT.Exp,
+                )
+            scores[t] = eb_grouped
+
+        def quantise_scores(t):
+            b, i = divmod(t, TILES_PER_BATCH)
+            if b not in score_codes:
+                eb_codes = codes.tile(
+                    [P, TILES_PER_BATCH, PASSES, P], U32, name="eb_codes", align_bytes=64
+                )
+                eb_scales = codes.tile(
+                    [P, TILES_PER_BATCH, PASSES, P], U8, name="eb_scales", align_bytes=64
+                )
+                score_codes[b] = (eb_codes, eb_scales)
+            eb_codes, eb_scales = score_codes[b]
+            nc.vector.quantize_mx(
+                out=eb_codes[:, i, :, :].rearrange("p g r -> p (g r)").bitcast(FP8X4),
+                scales=eb_scales[:, i, :, :].rearrange("p g r -> p (g r)"),
+                in_=scores[t][:].rearrange("p g r j -> p (g r j)"),
+            )
+
+        def copy_node_t(t, copy):
+            node_cols = stage.tile([P, F_CHUNKS, P], BF16, name="node_cols")
+            copy(out=node_cols[:], in_=node_ps[t][:])
+            node_t[t] = node_cols
+
+        def mix(t, kind):
+            b, i = divmod(t, TILES_PER_BATCH)
+            eb_codes, eb_scales = score_codes[b]
+            key_words, key_scales = key_codes[(b, kind)]
+            acc = psum_out.tile([P, D], F32, name="acc", tag="out_bank")
+            for g in range(PASSES):
+                nc.tensor.matmul_mx(
+                    out=acc[:],
+                    lhsT=eb_codes[:, i, g, :].bitcast(FP8X4),
+                    lhsT_scale=eb_scales[:, i, g, :],
+                    rhs=key_words[:, g, :].bitcast(FP8X4),
+                    rhs_scale=key_scales[:, g, :],
+                    start=(g == 0),
+                    stop=(g == PASSES - 1),
+                )
+            return acc
+
+        def tanh_gate(t):
+            gate_t = gates.tile([P, D], F32, name="gate_t")
+            nc.scalar.activation(out=gate_t[:], in_=q_ps[t][:], func=ACT.Tanh, scale=0.5)
+            gate[t] = gate_t
+
+        def merge_gate_and_num(t):
+            nc.vector.scalar_tensor_tensor(
+                out=gate[t][:], in0=gate[t][:], scalar=1.0, in1=num_ps[t][:],
+                op0=ALU.add, op1=ALU.mult,
+            )
+
+        def log_of_den(t):
+            den = mix(t, "ek")
+            log_t = logs.tile([P, D], F32, name="log_t")
+            nc.scalar.activation(out=log_t[:], in_=den[:], func=ACT.Ln)
+            log_den[t] = log_t
+
+        def reciprocal_of_den(t):
+            nc.scalar.activation(out=log_den[t][:], in_=log_den[t][:], func=ACT.Exp, scale=-1.0)
+
+        def finish(t):
+            b, i = divmod(t, TILES_PER_BATCH)
+            nc.vector.scalar_tensor_tensor(
+                out=gate[t][:], in0=gate[t][:], scalar=0.5, in1=log_den[t][:],
+                op0=ALU.mult, op1=ALU.mult,
+            )
+            nc.sync.dma_start(out=out_view[b, :, i, :], in_=gate[t][:])
+
+        load_rows = consts.tile([P, B * N], BF16, name="load_rows")
+        nc.vector.memset(load_rows[:], 0.0)
+
+        alpha_all = consts.tile([P, 1], BF16, name="alpha_all")
+        nc.sync.dma_start(out=alpha_all[:], in_=alpha1.partition_broadcast(P))
+        scale_all = consts.tile([P, 1], BF16, name="scale_all")
+        nc.sync.dma_start(out=scale_all[:], in_=log_scale.partition_broadcast(P))
+        for g in range(PASSES):
+            load_keys(0, g)
+        neg_slope = consts.tile([P, 1], F32, name="neg_slope")
+        nc.vector.scalar_tensor_tensor(
+            out=neg_slope[:], in0=alpha_all[:], scalar=-1.0, in1=scale_all[:],
+            op0=ALU.mult, op1=ALU.mult,
+        )
+
+        wq_rows = consts.tile([P, F_CHUNKS, D + 2], BF16, name="wq_rows")
+        nc.sync.dma_start(
+            out=wq_rows[:, :, 0 : D + 1], in_=Wq_last.rearrange("(r p) f -> p r f", p=P)
+        )
+        nc.sync.dma_start(
+            out=load_rows[P - 1 : P, :], in_=load.rearrange("(o b) n -> o (b n)", o=1)
+        )
+        load_by_tile = load_rows[:].rearrange("q (b p i) -> q b i p", b=B, i=TILES_PER_BATCH)
+
+        ident_f32 = consts.tile([P, P], F32, name="ident_f32")
+        make_identity(nc, ident_f32[:])
+        ident_bf16 = consts.tile([P, P], BF16, name="ident_bf16")
+        make_identity(nc, ident_bf16[:])
+
+        for piece in range(PIECES_PER_BATCH):
+            exp_keys(piece)
+        quantise_keys(0, "ekv")
+        quantise_keys(0, "ek")
+
+        wq_t = consts.tile([P, F_CHUNKS + 1, D], BF16, name="wq_t")
+        for c in range(F_CHUNKS + 1):
+            first = min(c * P, D + 1 - P)
+            wq_ps = psum_out.tile([P, F_CHUNKS, P], BF16, name="wq_ps", tag="out_bank")
+            for r in range(F_CHUNKS):
+                nc.tensor.transpose(
+                    wq_ps[:, r, :], wq_rows[:, r, first : first + P], ident_bf16[:]
+                )
+            nc.scalar.copy(out=wq_t[:, c, :], in_=wq_ps[:].rearrange("p r d -> p (r d)"))
+
+        for step in range(FIRST_STEP, LAST_STEP + 1):
+            key_load, rest = divmod(step + KEY_LOAD_LEAD, PIECES_PER_PASS)
+            if rest == 0 and PASSES <= key_load < B * PASSES:
+                load_keys(key_load // PASSES, key_load % PASSES)
+            query_load, rest = divmod(step + LOAD_LEAD, LOAD_TILES)
+            if rest == 0 and query_load < TILES // LOAD_TILES:
+                load_queries(query_load)
+
+            if is_tile(step + EXP_LEAD) and (step + EXP_LEAD) % 2 == 1:
+                copy_node_t(step + EXP_LEAD, nc.vector.tensor_copy)
+            if is_tile(step - MERGE_LAG):
+                merge_gate_and_num(step - MERGE_LAG)
+            if is_tile(step):
+                quantise_scores(step)
+            if is_tile(step + EXPONENT_LEAD):
+                form_exponents(step + EXPONENT_LEAD)
+            batch, rest = divmod(step, TILES_PER_BATCH)
+            if rest == 0 and 1 <= batch < B:
+                quantise_keys(batch, "ekv")
+                quantise_keys(batch, "ek")
+            if is_tile(step - FINISH_LAG):
+                finish(step - FINISH_LAG)
+
+            project_and_transpose(step, step + TRANSPOSE_LEAD)
+            if is_tile(step - NUM_LAG):
+                num_ps[step - NUM_LAG] = mix(step - NUM_LAG, "ekv")
+
+            if is_tile(step + EXP_LEAD) and (step + EXP_LEAD) % 2 == 0:
+                copy_node_t(step + EXP_LEAD, nc.scalar.copy)
+            if is_tile(step + EXP_LEAD):
+                exp_scores(step + EXP_LEAD)
+            if is_tile(step - NUM_LAG):
+                tanh_gate(step - NUM_LAG)
+            if PIECES_PER_BATCH <= step + KEY_LEAD < PIECES:
+                exp_keys(step + KEY_LEAD)
+            if is_tile(step - RECIP_LAG):
+                reciprocal_of_den(step - RECIP_LAG)
+
+            batch, rest = divmod(step + 1, TILES_PER_BATCH)
+            if rest == 0 and 1 <= batch <= B:
+                for t in range((batch - 1) * TILES_PER_BATCH, batch * TILES_PER_BATCH):
+                    log_of_den(t)

@@ -20,7 +20,7 @@ K_PASS = P * PACK
 PASSES = M // K_PASS
 TILES_PER_BATCH = N // P
 TILES = B * TILES_PER_BATCH
-LOAD_TILES = TILES_PER_BATCH // 2
+LOAD_TILES = 2
 F_CHUNKS = D // P
 T_PER_MATMUL = (M // P + F_CHUNKS) // F_CHUNKS
 PIECE = P
@@ -60,7 +60,7 @@ def tile_cvrp_decoder_pa_t_kernel(
     with ExitStack() as ctx:
         ctx.enter_context(tc.manual_schedule())
         consts = ctx.enter_context(tc.tile_pool(name="consts", bufs=1))
-        loads = ctx.enter_context(tc.tile_pool(name="loads", bufs=2))
+        loads = ctx.enter_context(tc.tile_pool(name="loads", bufs=4))
         values = ctx.enter_context(tc.tile_pool(name="values", bufs=2 * PASSES))
         codes = ctx.enter_context(tc.tile_pool(name="codes", bufs=2))
         stage = ctx.enter_context(tc.tile_pool(name="stage", bufs=3))
@@ -234,11 +234,11 @@ def tile_cvrp_decoder_pa_t_kernel(
             copy(out=node_cols[:], in_=node_ps[t][:])
             node_t[t] = node_cols
 
-        def mix(t, kind):
+        def mix(t, kind, pool=psum_out, tag="out_bank"):
             b, i = divmod(t, TILES_PER_BATCH)
             eb_codes, eb_scales = score_codes[b]
             key_words, key_scales = key_codes[(b, kind)]
-            acc = psum_out.tile([P, D], F32, name="acc", tag="out_bank")
+            acc = pool.tile([P, D], F32, name="acc", tag=tag)
             for g in range(PASSES):
                 nc.tensor.matmul_mx(
                     out=acc[:],
@@ -261,6 +261,12 @@ def tile_cvrp_decoder_pa_t_kernel(
                 out=gate[t][:], in0=gate[t][:], scalar=1.0, in1=num_ps[t][:],
                 op0=ALU.add, op1=ALU.mult,
             )
+
+        def reciprocal_by_vector(t):
+            den = mix(t, "ek", psum_xt, "xt")
+            log_t = logs.tile([P, D], F32, name="log_t")
+            nc.vector.reciprocal(out=log_t[:], in_=den[:])
+            log_den[t] = log_t
 
         def log_of_den(t):
             den = mix(t, "ek")
@@ -303,6 +309,8 @@ def tile_cvrp_decoder_pa_t_kernel(
         )
         load_by_tile = load_rows[:].rearrange("q (b p i) -> q b i p", b=B, i=TILES_PER_BATCH)
 
+        load_queries(0)
+
         ident_f32 = consts.tile([P, P], F32, name="ident_f32")
         make_identity(nc, ident_f32[:])
         ident_bf16 = consts.tile([P, P], BF16, name="ident_bf16")
@@ -311,6 +319,7 @@ def tile_cvrp_decoder_pa_t_kernel(
         for piece in range(PIECES_PER_BATCH):
             exp_keys(piece)
         quantise_keys(0, "ekv")
+        form_exponents(0)
         quantise_keys(0, "ek")
 
         wq_t = consts.tile([P, F_CHUNKS + 1, D], BF16, name="wq_t")
@@ -328,16 +337,16 @@ def tile_cvrp_decoder_pa_t_kernel(
             if rest == 0 and PASSES <= key_load < B * PASSES:
                 load_keys(key_load // PASSES, key_load % PASSES)
             query_load, rest = divmod(step + LOAD_LEAD, LOAD_TILES)
-            if rest == 0 and query_load < TILES // LOAD_TILES:
+            if rest == 0 and 0 < query_load < TILES // LOAD_TILES:
                 load_queries(query_load)
 
             if is_tile(step + EXP_LEAD) and (step + EXP_LEAD) % 2 == 1:
                 copy_node_t(step + EXP_LEAD, nc.vector.tensor_copy)
-            if is_tile(step - MERGE_LAG):
+            if is_tile(step - MERGE_LAG) and step - MERGE_LAG != TILES - 2:
                 merge_gate_and_num(step - MERGE_LAG)
             if is_tile(step):
                 quantise_scores(step)
-            if is_tile(step + EXPONENT_LEAD):
+            if is_tile(step + EXPONENT_LEAD) and step + EXPONENT_LEAD > 0:
                 form_exponents(step + EXPONENT_LEAD)
             batch, rest = divmod(step, TILES_PER_BATCH)
             if rest == 0 and 1 <= batch < B:
@@ -354,14 +363,20 @@ def tile_cvrp_decoder_pa_t_kernel(
                 copy_node_t(step + EXP_LEAD, nc.scalar.copy)
             if is_tile(step + EXP_LEAD):
                 exp_scores(step + EXP_LEAD)
-            if is_tile(step - NUM_LAG):
+            if is_tile(step - NUM_LAG) and step - NUM_LAG < TILES - 1:
                 tanh_gate(step - NUM_LAG)
             if PIECES_PER_BATCH <= step + KEY_LEAD < PIECES:
                 exp_keys(step + KEY_LEAD)
-            if is_tile(step - RECIP_LAG):
+            if is_tile(step - RECIP_LAG) and step - RECIP_LAG != TILES - TILES_PER_BATCH:
                 reciprocal_of_den(step - RECIP_LAG)
 
             batch, rest = divmod(step + 1, TILES_PER_BATCH)
             if rest == 0 and 1 <= batch <= B:
-                for t in range((batch - 1) * TILES_PER_BATCH, batch * TILES_PER_BATCH):
+                first = (batch - 1) * TILES_PER_BATCH
+                if batch == B:
+                    tanh_gate(step)
+                    merge_gate_and_num(step - 1)
+                    reciprocal_by_vector(first)
+                    first += 1
+                for t in range(first, batch * TILES_PER_BATCH):
                     log_of_den(t)

@@ -50,10 +50,10 @@ def tile_cvrp_decoder_pa_t_kernel(
 ):
     nc = tc.nc
 
-    dist_view = cur_dist.rearrange("b (p i) m -> b p i m", i=TILES_PER_BATCH)
-    mask_view = ninf_mask.rearrange("b (p i) m -> b p i m", i=TILES_PER_BATCH)
-    node_view = encoded_last_node.rearrange("b (p i) f -> b p i f", i=TILES_PER_BATCH)
-    out_view = out.rearrange("b (p i) d -> b p i d", i=TILES_PER_BATCH)
+    dist_view = cur_dist.rearrange("b (i p) m -> b p i m", i=TILES_PER_BATCH)
+    mask_view = ninf_mask.rearrange("b (i p) m -> b p i m", i=TILES_PER_BATCH)
+    node_view = encoded_last_node.rearrange("b (i p) f -> b p i f", i=TILES_PER_BATCH)
+    out_view = out.rearrange("b (i p) d -> b p i d", i=TILES_PER_BATCH)
     k_view = k.rearrange("b (g p j) d -> b g p j d", g=PASSES, j=PACK)
     v_view = v.rearrange("b (g p j) d -> b g p j d", g=PASSES, j=PACK)
 
@@ -102,7 +102,10 @@ def tile_cvrp_decoder_pa_t_kernel(
 
         def load_keys(b, g):
             k_rows = loads.tile([P, PACK, D], BF16, name="k_rows")
-            nc.sync.dma_start(out=k_rows[:], in_=k_view[b, g])
+            halves = 2 if b == 0 and g == 0 else 1
+            for h in range(halves):
+                js = slice(h * PACK // halves, (h + 1) * PACK // halves)
+                nc.sync.dma_start(out=k_rows[:, js, :], in_=k_view[b, g, :, js, :])
             v_rows = values.tile([P, PACK, D], BF16, name="v_rows")
             nc.sync.dma_start(out=v_rows[:], in_=v_view[b, g])
             key_loads[(b, g)] = (k_rows, v_rows)
@@ -274,31 +277,35 @@ def tile_cvrp_decoder_pa_t_kernel(
             nc.scalar.activation(out=log_t[:], in_=den[:], func=ACT.Ln)
             log_den[t] = log_t
 
+        def columns(t):
+            width = D // 2 if t == TILES - 1 else D
+            return [slice(first, first + width) for first in range(0, D, width)]
+
         def reciprocal_of_den(t):
-            nc.scalar.activation(out=log_den[t][:], in_=log_den[t][:], func=ACT.Exp, scale=-1.0)
+            for cols in columns(t):
+                part = log_den[t][:, cols]
+                nc.scalar.activation(out=part, in_=part, func=ACT.Exp, scale=-1.0)
 
         def finish(t):
             b, i = divmod(t, TILES_PER_BATCH)
-            nc.vector.scalar_tensor_tensor(
-                out=gate[t][:], in0=gate[t][:], scalar=0.5, in1=log_den[t][:],
-                op0=ALU.mult, op1=ALU.mult,
-            )
-            nc.sync.dma_start(out=out_view[b, :, i, :], in_=gate[t][:])
+            for cols in columns(t):
+                part = gate[t][:, cols]
+                nc.vector.scalar_tensor_tensor(
+                    out=part, in0=part, scalar=0.5, in1=log_den[t][:, cols],
+                    op0=ALU.mult, op1=ALU.mult,
+                )
+                nc.sync.dma_start(out=out_view[b, :, i, cols], in_=part)
 
         load_rows = consts.tile([P, B * N], BF16, name="load_rows")
         nc.vector.memset(load_rows[:], 0.0)
 
+        for g in range(PASSES):
+            load_keys(0, g)
         alpha_all = consts.tile([P, 1], BF16, name="alpha_all")
         nc.sync.dma_start(out=alpha_all[:], in_=alpha1.partition_broadcast(P))
         scale_all = consts.tile([P, 1], BF16, name="scale_all")
         nc.sync.dma_start(out=scale_all[:], in_=log_scale.partition_broadcast(P))
-        for g in range(PASSES):
-            load_keys(0, g)
         neg_slope = consts.tile([P, 1], F32, name="neg_slope")
-        nc.vector.scalar_tensor_tensor(
-            out=neg_slope[:], in0=alpha_all[:], scalar=-1.0, in1=scale_all[:],
-            op0=ALU.mult, op1=ALU.mult,
-        )
 
         wq_rows = consts.tile([P, F_CHUNKS, D + 2], BF16, name="wq_rows")
         nc.sync.dma_start(
@@ -307,7 +314,7 @@ def tile_cvrp_decoder_pa_t_kernel(
         nc.sync.dma_start(
             out=load_rows[P - 1 : P, :], in_=load.rearrange("(o b) n -> o (b n)", o=1)
         )
-        load_by_tile = load_rows[:].rearrange("q (b p i) -> q b i p", b=B, i=TILES_PER_BATCH)
+        load_by_tile = load_rows[:].rearrange("q (b i p) -> q b i p", b=B, i=TILES_PER_BATCH)
 
         load_queries(0)
 
@@ -316,9 +323,18 @@ def tile_cvrp_decoder_pa_t_kernel(
         ident_bf16 = consts.tile([P, P], BF16, name="ident_bf16")
         make_identity(nc, ident_bf16[:])
 
-        for piece in range(PIECES_PER_BATCH):
-            exp_keys(piece)
+        for g in range(PASSES):
+            ek = stage.tile([P, PACK, D], F32, name="ek")
+            key_exp[(0, g)] = ek
+            for j in range(PACK):
+                nc.scalar.activation(
+                    out=ek[:, j, :], in_=key_loads[(0, g)][0][:, j, :], func=ACT.Exp
+                )
         quantise_keys(0, "ekv")
+        nc.vector.scalar_tensor_tensor(
+            out=neg_slope[:], in0=alpha_all[:], scalar=-1.0, in1=scale_all[:],
+            op0=ALU.mult, op1=ALU.mult,
+        )
         form_exponents(0)
         quantise_keys(0, "ek")
 

@@ -358,19 +358,19 @@ def tile_cvrp_decoder_pa_t_kernel(
 
             if is_tile(step + EXP_LEAD) and (step + EXP_LEAD) % 2 == 1:
                 copy_node_t(step + EXP_LEAD, nc.vector.tensor_copy)
-            if is_tile(step - MERGE_LAG) and step - MERGE_LAG != TILES - 2:
-                merge_gate_and_num(step - MERGE_LAG)
-            if is_tile(step):
-                quantise_scores(step)
             if is_tile(step + EXPONENT_LEAD) and step + EXPONENT_LEAD > 0:
                 form_exponents(step + EXPONENT_LEAD)
+            if is_tile(step):
+                quantise_scores(step)
+            if is_tile(step - MERGE_LAG) and step - MERGE_LAG != TILES - 2:
+                merge_gate_and_num(step - MERGE_LAG)
+            if is_tile(step - FINISH_LAG):
+                finish(step - FINISH_LAG)
+
             batch, rest = divmod(step, TILES_PER_BATCH)
             if rest == 0 and 1 <= batch < B:
                 quantise_keys(batch, "ekv")
                 quantise_keys(batch, "ek")
-            if is_tile(step - FINISH_LAG):
-                finish(step - FINISH_LAG)
-
             project_and_transpose(step, step + TRANSPOSE_LEAD)
             if is_tile(step - NUM_LAG):
                 num_ps[step - NUM_LAG] = mix(step - NUM_LAG, "ekv")

@@ -41,6 +41,9 @@ DMA_STEPS = 3
 LOAD_LEAD = EXPONENT_LEAD + DMA_STEPS
 KEY_LEAD = PIECES_PER_BATCH
 KEY_LOAD_LEAD = KEY_LEAD + DMA_STEPS
+VECTOR_COLUMNS = {TILES - TILES_PER_BATCH: D, TILES - TILES_PER_BATCH + 1: D // 4}
+HALVES = (slice(0, D // 2), slice(D // 2, D))
+VALUE_LEAD = 5
 FIRST_STEP = -LOAD_LEAD
 LAST_STEP = TILES - 1 + FINISH_LAG
 
@@ -72,6 +75,7 @@ def tile_cvrp_decoder_pa_t_kernel(
         psum_out = ctx.enter_context(tc.psum_pool(name="psum_out", bufs=4))
 
         query_loads = {}
+        value_loads = {}
         key_loads = {}
         key_exp = {}
         key_codes = {}
@@ -84,6 +88,7 @@ def tile_cvrp_decoder_pa_t_kernel(
         q_ps = {}
         num_ps = {}
         gate = {}
+        den_ps = {}
         log_den = {}
 
         def is_tile(t):
@@ -106,9 +111,12 @@ def tile_cvrp_decoder_pa_t_kernel(
             for h in range(halves):
                 js = slice(h * PACK // halves, (h + 1) * PACK // halves)
                 nc.sync.dma_start(out=k_rows[:, js, :], in_=k_view[b, g, :, js, :])
+            key_loads[(b, g)] = k_rows
+
+        def load_values(b, g):
             v_rows = values.tile([P, PACK, D], BF16, name="v_rows")
             nc.sync.dma_start(out=v_rows[:], in_=v_view[b, g])
-            key_loads[(b, g)] = (k_rows, v_rows)
+            value_loads[(b, g)] = v_rows
 
         def exp_keys(piece):
             b, rest = divmod(piece, PIECES_PER_BATCH)
@@ -118,7 +126,7 @@ def tile_cvrp_decoder_pa_t_kernel(
                 key_exp[(b, g)] = ek
             cols = slice(part * PIECE, (part + 1) * PIECE)
             nc.scalar.activation(
-                out=key_exp[(b, g)][:, :, cols], in_=key_loads[(b, g)][0][:, :, cols], func=ACT.Exp
+                out=key_exp[(b, g)][:, :, cols], in_=key_loads[(b, g)][:, :, cols], func=ACT.Exp
             )
 
         def quantise_keys(b, kind):
@@ -131,8 +139,15 @@ def tile_cvrp_decoder_pa_t_kernel(
                 out_runs = in_order[:].rearrange("p (a e) j -> p a j e", e=RUN)
                 ek_runs = key_exp[(b, g)][:].rearrange("p j (a e) -> p a j e", e=RUN)
                 if kind == "ekv":
-                    v_runs = key_loads[(b, g)][1][:].rearrange("p j (a e) -> p a j e", e=RUN)
-                    nc.vector.tensor_tensor(out=out_runs, in0=ek_runs, in1=v_runs, op=ALU.mult)
+                    v_runs = value_loads[(b, g)][:].rearrange("p j (a e) -> p a j e", e=RUN)
+                    runs = D // RUN
+                    parts = 2 if b == 0 else 1
+                    for h in range(parts):
+                        some = slice(h * runs // parts, (h + 1) * runs // parts)
+                        nc.vector.tensor_tensor(
+                            out=out_runs[:, some], in0=ek_runs[:, some], in1=v_runs[:, some],
+                            op=ALU.mult,
+                        )
                 elif b == 0:
                     nc.scalar.copy(out=out_runs, in_=ek_runs)
                 else:
@@ -265,24 +280,27 @@ def tile_cvrp_decoder_pa_t_kernel(
                 op0=ALU.add, op1=ALU.mult,
             )
 
-        def reciprocal_by_vector(t):
-            den = mix(t, "ek", psum_xt, "xt")
-            log_t = logs.tile([P, D], F32, name="log_t")
-            nc.vector.reciprocal(out=log_t[:], in_=den[:])
-            log_den[t] = log_t
-
         def log_of_den(t):
-            den = mix(t, "ek")
+            by_vector = VECTOR_COLUMNS.get(t, 0)
+            den = mix(t, "ek", psum_xt, "xt") if by_vector else mix(t, "ek")
             log_t = logs.tile([P, D], F32, name="log_t")
-            nc.scalar.activation(out=log_t[:], in_=den[:], func=ACT.Ln)
+            if by_vector < D:
+                nc.scalar.activation(
+                    out=log_t[:, by_vector:], in_=den[:, by_vector:], func=ACT.Ln
+                )
+            den_ps[t] = den
             log_den[t] = log_t
 
-        def columns(t):
-            width = D // 2 if t == TILES - 1 else D
-            return [slice(first, first + width) for first in range(0, D, width)]
+        def reciprocal_by_vector(t):
+            cols = slice(0, VECTOR_COLUMNS[t])
+            nc.vector.reciprocal(out=log_den[t][:, cols], in_=den_ps[t][:, cols])
+
+        def columns(t, first=0):
+            width = D // 2 if t == TILES - 1 else D - first
+            return [slice(c, c + width) for c in range(first, D, width)] if first < D else []
 
         def reciprocal_of_den(t):
-            for cols in columns(t):
+            for cols in columns(t, VECTOR_COLUMNS.get(t, 0)):
                 part = log_den[t][:, cols]
                 nc.scalar.activation(out=part, in_=part, func=ACT.Exp, scale=-1.0)
 
@@ -301,6 +319,7 @@ def tile_cvrp_decoder_pa_t_kernel(
 
         for g in range(PASSES):
             load_keys(0, g)
+            load_values(0, g)
         alpha_all = consts.tile([P, 1], BF16, name="alpha_all")
         nc.sync.dma_start(out=alpha_all[:], in_=alpha1.partition_broadcast(P))
         scale_all = consts.tile([P, 1], BF16, name="scale_all")
@@ -326,10 +345,11 @@ def tile_cvrp_decoder_pa_t_kernel(
         for g in range(PASSES):
             ek = stage.tile([P, PACK, D], F32, name="ek")
             key_exp[(0, g)] = ek
-            for j in range(PACK):
-                nc.scalar.activation(
-                    out=ek[:, j, :], in_=key_loads[(0, g)][0][:, j, :], func=ACT.Exp
-                )
+            for cols in HALVES:
+                for js in (slice(0, PACK // 2), slice(PACK // 2, PACK)):
+                    nc.scalar.activation(
+                        out=ek[:, js, cols], in_=key_loads[(0, g)][:, js, cols], func=ACT.Exp
+                    )
         quantise_keys(0, "ekv")
         nc.vector.scalar_tensor_tensor(
             out=neg_slope[:], in0=alpha_all[:], scalar=-1.0, in1=scale_all[:],
@@ -352,6 +372,9 @@ def tile_cvrp_decoder_pa_t_kernel(
             key_load, rest = divmod(step + KEY_LOAD_LEAD, PIECES_PER_PASS)
             if rest == 0 and PASSES <= key_load < B * PASSES:
                 load_keys(key_load // PASSES, key_load % PASSES)
+            batch, g = divmod(step + VALUE_LEAD, TILES_PER_BATCH)
+            if 1 <= batch < B and g < PASSES:
+                load_values(batch, g)
             query_load, rest = divmod(step + LOAD_LEAD, LOAD_TILES)
             if rest == 0 and 0 < query_load < TILES // LOAD_TILES:
                 load_queries(query_load)
@@ -366,12 +389,17 @@ def tile_cvrp_decoder_pa_t_kernel(
                 merge_gate_and_num(step - MERGE_LAG)
             if is_tile(step - FINISH_LAG):
                 finish(step - FINISH_LAG)
+            if step == TILES + 1:
+                reciprocal_by_vector(TILES - TILES_PER_BATCH + 1)
 
             batch, rest = divmod(step, TILES_PER_BATCH)
             if rest == 0 and 1 <= batch < B:
                 quantise_keys(batch, "ekv")
                 quantise_keys(batch, "ek")
-            project_and_transpose(step, step + TRANSPOSE_LEAD)
+            if step != TILES - 1:
+                project_and_transpose(step, step + TRANSPOSE_LEAD)
+            if step == TILES - 2:
+                project_and_transpose(step + 1, TILES)
             if is_tile(step - NUM_LAG):
                 num_ps[step - NUM_LAG] = mix(step - NUM_LAG, "ekv")
 
@@ -383,7 +411,7 @@ def tile_cvrp_decoder_pa_t_kernel(
                 tanh_gate(step - NUM_LAG)
             if PIECES_PER_BATCH <= step + KEY_LEAD < PIECES:
                 exp_keys(step + KEY_LEAD)
-            if is_tile(step - RECIP_LAG) and step - RECIP_LAG != TILES - TILES_PER_BATCH:
+            if is_tile(step - RECIP_LAG):
                 reciprocal_of_den(step - RECIP_LAG)
 
             batch, rest = divmod(step + 1, TILES_PER_BATCH)
@@ -392,7 +420,7 @@ def tile_cvrp_decoder_pa_t_kernel(
                 if batch == B:
                     tanh_gate(step)
                     merge_gate_and_num(step - 1)
-                    reciprocal_by_vector(first)
-                    first += 1
                 for t in range(first, batch * TILES_PER_BATCH):
                     log_of_den(t)
+                if batch == B:
+                    reciprocal_by_vector(TILES - TILES_PER_BATCH)

from contextlib import ExitStack

import concourse.mybir as mybir
from concourse.masks import make_identity

F32 = mybir.dt.float32
BF16 = mybir.dt.bfloat16
U32 = mybir.dt.uint32
U8 = mybir.dt.uint8
FP8X4 = mybir.dt.float8_e4m3fn_x4
ACT = mybir.ActivationFunctionType
ALU = mybir.AluOpType

B, N, M, D = 4, 1024, 1024, 512
FLOPS = 2 * B * N * D * (D + 1) + 2 * 2 * B * N * M * D

P = 128
PACK = 4
K_PASS = P * PACK
PASSES = M // K_PASS
TILES_PER_BATCH = N // P
TILES = B * TILES_PER_BATCH
LOAD_TILES = 2
F_CHUNKS = D // P
T_PER_MATMUL = (M // P + F_CHUNKS) // F_CHUNKS
PIECE = P
PIECES_PER_PASS = D // PIECE
PIECES_PER_BATCH = PASSES * PIECES_PER_PASS
PIECES = B * PIECES_PER_BATCH
assert PIECES_PER_BATCH == TILES_PER_BATCH
RUN = 4

EXPONENT_LEAD = 3
TRANSPOSE_LEAD = 2
EXP_LEAD = 1
NUM_LAG = 1
MERGE_LAG = 2
RECIP_LAG = TILES_PER_BATCH
FINISH_LAG = RECIP_LAG + 1
DMA_STEPS = 3
LOAD_LEAD = EXPONENT_LEAD + DMA_STEPS
KEY_LEAD = PIECES_PER_BATCH
KEY_LOAD_LEAD = KEY_LEAD + DMA_STEPS
VECTOR_COLUMNS = {TILES - TILES_PER_BATCH: D, TILES - TILES_PER_BATCH + 1: D // 4}
HALVES = (slice(0, D // 2), slice(D // 2, D))
VALUE_LEAD = 5
FIRST_STEP = -LOAD_LEAD
LAST_STEP = TILES - 1 + FINISH_LAG


def tile_cvrp_decoder_pa_t_kernel(
    tc, encoded_last_node, load, cur_dist, log_scale, ninf_mask, k, v, Wq_last, alpha1, out
):
    nc = tc.nc

    dist_view = cur_dist.rearrange("b (i p) m -> b p i m", i=TILES_PER_BATCH)
    mask_view = ninf_mask.rearrange("b (i p) m -> b p i m", i=TILES_PER_BATCH)
    node_view = encoded_last_node.rearrange("b (i p) f -> b p i f", i=TILES_PER_BATCH)
    out_view = out.rearrange("b (i p) d -> b p i d", i=TILES_PER_BATCH)
    k_view = k.rearrange("b (g p j) d -> b g p j d", g=PASSES, j=PACK)
    v_view = v.rearrange("b (g p j) d -> b g p j d", g=PASSES, j=PACK)

    with ExitStack() as ctx:
        ctx.enter_context(tc.manual_schedule())
        consts = ctx.enter_context(tc.tile_pool(name="consts", bufs=1))
        loads = ctx.enter_context(tc.tile_pool(name="loads", bufs=4))
        values = ctx.enter_context(tc.tile_pool(name="values", bufs=2 * PASSES))
        codes = ctx.enter_context(tc.tile_pool(name="codes", bufs=2))
        stage = ctx.enter_context(tc.tile_pool(name="stage", bufs=3))
        grouped = ctx.enter_context(tc.tile_pool(name="grouped", bufs=PASSES))
        gates = ctx.enter_context(tc.tile_pool(name="gates", bufs=FINISH_LAG + 2))
        logs = ctx.enter_context(tc.tile_pool(name="logs", bufs=TILES_PER_BATCH + 2))
        psum_xt = ctx.enter_context(tc.psum_pool(name="psum_xt", bufs=3))
        psum_et = ctx.enter_context(tc.psum_pool(name="psum_et", bufs=1))
        psum_out = ctx.enter_context(tc.psum_pool(name="psum_out", bufs=4))

        query_loads = {}
        value_loads = {}
        key_loads = {}
        key_exp = {}
        key_codes = {}
        score_codes = {}
        exponents = {}
        transposed = {}
        scores = {}
        node_ps = {}
        node_t = {}
        q_ps = {}
        num_ps = {}
        gate = {}
        den_ps = {}
        log_den = {}

        def is_tile(t):
            return 0 <= t < TILES

        def load_queries(h):
            b, first = divmod(h * LOAD_TILES, TILES_PER_BATCH)
            rows = slice(first, first + LOAD_TILES)
            dist = loads.tile([P, LOAD_TILES, M], BF16, name="dist")
            nc.sync.dma_start(out=dist[:], in_=dist_view[b, :, rows, :])
            mask = loads.tile([P, LOAD_TILES, M], BF16, name="mask")
            nc.sync.dma_start(out=mask[:], in_=mask_view[b, :, rows, :])
            node = loads.tile([P, LOAD_TILES, D], BF16, name="node")
            nc.sync.dma_start(out=node[:], in_=node_view[b, :, rows, :])
            query_loads[h] = (dist, mask, node)

        def load_keys(b, g):
            k_rows = loads.tile([P, PACK, D], BF16, name="k_rows")
            halves = 2 if b == 0 and g == 0 else 1
            for h in range(halves):
                js = slice(h * PACK // halves, (h + 1) * PACK // halves)
                nc.sync.dma_start(out=k_rows[:, js, :], in_=k_view[b, g, :, js, :])
            key_loads[(b, g)] = k_rows

        def load_values(b, g):
            v_rows = values.tile([P, PACK, D], BF16, name="v_rows")
            nc.sync.dma_start(out=v_rows[:], in_=v_view[b, g])
            value_loads[(b, g)] = v_rows

        def exp_keys(piece):
            b, rest = divmod(piece, PIECES_PER_BATCH)
            g, part = divmod(rest, PIECES_PER_PASS)
            if part == 0:
                ek = stage.tile([P, PACK, D], F32, name="ek")
                key_exp[(b, g)] = ek
            cols = slice(part * PIECE, (part + 1) * PIECE)
            nc.scalar.activation(
                out=key_exp[(b, g)][:, :, cols], in_=key_loads[(b, g)][:, :, cols], func=ACT.Exp
            )

        def quantise_keys(b, kind):
            words = codes.tile([P, PASSES, D], U32, name="%s_words" % kind, align_bytes=64)
            scales = codes.tile([P, PASSES, D], U8, name="%s_scales" % kind, align_bytes=64)
            key_codes[(b, kind)] = (words, scales)
            rounded = []
            for g in range(PASSES):
                in_order = grouped.tile([P, D, PACK], BF16, name="%s_in_order" % kind, align_bytes=64)
                out_runs = in_order[:].rearrange("p (a e) j -> p a j e", e=RUN)
                ek_runs = key_exp[(b, g)][:].rearrange("p j (a e) -> p a j e", e=RUN)
                if kind == "ekv":
                    v_runs = value_loads[(b, g)][:].rearrange("p j (a e) -> p a j e", e=RUN)
                    runs = D // RUN
                    parts = 2 if b == 0 else 1
                    for h in range(parts):
                        some = slice(h * runs // parts, (h + 1) * runs // parts)
                        nc.vector.tensor_tensor(
                            out=out_runs[:, some], in0=ek_runs[:, some], in1=v_runs[:, some],
                            op=ALU.mult,
                        )
                elif b == 0:
                    nc.scalar.copy(out=out_runs, in_=ek_runs)
                else:
                    nc.vector.tensor_copy(out=out_runs, in_=ek_runs)
                rounded.append(in_order)
            for g in range(PASSES):
                nc.vector.quantize_mx(
                    out=words[:, g, :].bitcast(FP8X4),
                    scales=scales[:, g, :],
                    in_=rounded[g][:].rearrange("p d j -> p (d j)"),
                )

        def form_exponents(t):
            dist, mask = query_loads[t // LOAD_TILES][0:2]
            row = t % LOAD_TILES
            exponent = stage.tile([P, PACK, M // PACK], F32, name="exponent")
            nc.vector.scalar_tensor_tensor(
                out=exponent[:],
                in0=dist[:, row, :].rearrange("p (w j) -> p j w", j=PACK),
                scalar=neg_slope[:, 0:1],
                in1=mask[:, row, :].rearrange("p (w j) -> p j w", j=PACK),
                op0=ALU.mult, op1=ALU.add,
            )
            exponents[t] = exponent

        def transposes_for(t):
            node = query_loads[t // LOAD_TILES][2]
            row = t % LOAD_TILES
            xts = []
            for g in range(PASSES):
                xt = psum_xt.tile([P, PACK, P], F32, name="xt")
                xts.append(xt)
            et = psum_et.tile([P, F_CHUNKS, P], BF16, name="et")
            transposed[t] = xts
            node_ps[t] = et

            def exponent_block(g, j):
                return lambda: nc.tensor.transpose(
                    xts[g][:, j, :], exponents[t][:, j, g * P : (g + 1) * P], ident_f32[:]
                )

            def node_block(c):
                return lambda: nc.tensor.transpose(
                    et[:, c, :], node[:, row, c * P : (c + 1) * P], ident_bf16[:]
                )

            return (
                [exponent_block(0, j) for j in range(PACK)]
                + [node_block(c) for c in range(F_CHUNKS)]
                + [exponent_block(1, j) for j in range(PACK)]
            )

        def project_and_transpose(t_q, t_next):
            waiting = transposes_for(t_next) if is_tile(t_next) else []
            if is_tile(t_q):
                b, i = divmod(t_q, TILES_PER_BATCH)
                q_acc = psum_out.tile([P, D], F32, name="q_acc", tag="out_bank")
                q_ps[t_q] = q_acc
            for c in range(F_CHUNKS):
                if is_tile(t_q):
                    nc.tensor.matmul(
                        out=q_acc[:], lhsT=node_t[t_q][:, c, :], rhs=wq_t[:, c, :],
                        start=(c == 0), stop=False,
                    )
                for transpose_block in waiting[c * T_PER_MATMUL : (c + 1) * T_PER_MATMUL]:
                    transpose_block()
            if is_tile(t_q):
                nc.tensor.matmul(
                    out=q_acc[:], lhsT=load_by_tile[:, b, i, :], rhs=wq_t[:, F_CHUNKS, :],
                    start=False, stop=True,
                )

        def exp_scores(t):
            eb_grouped = stage.tile([P, PASSES, P, PACK], BF16, name="eb_grouped", align_bytes=64)
            for g in range(PASSES):
                nc.scalar.activation(
                    out=eb_grouped[:, g, :, :],
                    in_=transposed[t][g][:].rearrange("p j r -> p r j"),
                    func=ACT.Exp,
                )
            scores[t] = eb_grouped

        def quantise_scores(t):
            b, i = divmod(t, TILES_PER_BATCH)
            if b not in score_codes:
                eb_codes = codes.tile(
                    [P, TILES_PER_BATCH, PASSES, P], U32, name="eb_codes", align_bytes=64
                )
                eb_scales = codes.tile(
                    [P, TILES_PER_BATCH, PASSES, P], U8, name="eb_scales", align_bytes=64
                )
                score_codes[b] = (eb_codes, eb_scales)
            eb_codes, eb_scales = score_codes[b]
            nc.vector.quantize_mx(
                out=eb_codes[:, i, :, :].rearrange("p g r -> p (g r)").bitcast(FP8X4),
                scales=eb_scales[:, i, :, :].rearrange("p g r -> p (g r)"),
                in_=scores[t][:].rearrange("p g r j -> p (g r j)"),
            )

        def copy_node_t(t, copy):
            node_cols = stage.tile([P, F_CHUNKS, P], BF16, name="node_cols")
            copy(out=node_cols[:], in_=node_ps[t][:])
            node_t[t] = node_cols

        def mix(t, kind, pool=psum_out, tag="out_bank"):
            b, i = divmod(t, TILES_PER_BATCH)
            eb_codes, eb_scales = score_codes[b]
            key_words, key_scales = key_codes[(b, kind)]
            acc = pool.tile([P, D], F32, name="acc", tag=tag)
            for g in range(PASSES):
                nc.tensor.matmul_mx(
                    out=acc[:],
                    lhsT=eb_codes[:, i, g, :].bitcast(FP8X4),
                    lhsT_scale=eb_scales[:, i, g, :],
                    rhs=key_words[:, g, :].bitcast(FP8X4),
                    rhs_scale=key_scales[:, g, :],
                    start=(g == 0),
                    stop=(g == PASSES - 1),
                )
            return acc

        def tanh_gate(t):
            gate_t = gates.tile([P, D], F32, name="gate_t")
            nc.scalar.activation(out=gate_t[:], in_=q_ps[t][:], func=ACT.Tanh, scale=0.5)
            gate[t] = gate_t

        def merge_gate_and_num(t):
            nc.vector.scalar_tensor_tensor(
                out=gate[t][:], in0=gate[t][:], scalar=1.0, in1=num_ps[t][:],
                op0=ALU.add, op1=ALU.mult,
            )

        def log_of_den(t):
            by_vector = VECTOR_COLUMNS.get(t, 0)
            den = mix(t, "ek", psum_xt, "xt") if by_vector else mix(t, "ek")
            log_t = logs.tile([P, D], F32, name="log_t")
            if by_vector < D:
                nc.scalar.activation(
                    out=log_t[:, by_vector:], in_=den[:, by_vector:], func=ACT.Ln
                )
            den_ps[t] = den
            log_den[t] = log_t

        def reciprocal_by_vector(t):
            cols = slice(0, VECTOR_COLUMNS[t])
            nc.vector.reciprocal(out=log_den[t][:, cols], in_=den_ps[t][:, cols])

        def columns(t, first=0):
            width = D // 2 if t == TILES - 1 else D - first
            return [slice(c, c + width) for c in range(first, D, width)] if first < D else []

        def reciprocal_of_den(t):
            for cols in columns(t, VECTOR_COLUMNS.get(t, 0)):
                part = log_den[t][:, cols]
                nc.scalar.activation(out=part, in_=part, func=ACT.Exp, scale=-1.0)

        def finish(t):
            b, i = divmod(t, TILES_PER_BATCH)
            for cols in columns(t):
                part = gate[t][:, cols]
                nc.vector.scalar_tensor_tensor(
                    out=part, in0=part, scalar=0.5, in1=log_den[t][:, cols],
                    op0=ALU.mult, op1=ALU.mult,
                )
                nc.sync.dma_start(out=out_view[b, :, i, cols], in_=part)

        load_rows = consts.tile([P, B * N], BF16, name="load_rows")
        nc.vector.memset(load_rows[:], 0.0)

        for g in range(PASSES):
            load_keys(0, g)
            load_values(0, g)
        alpha_all = consts.tile([P, 1], BF16, name="alpha_all")
        nc.sync.dma_start(out=alpha_all[:], in_=alpha1.partition_broadcast(P))
        scale_all = consts.tile([P, 1], BF16, name="scale_all")
        nc.sync.dma_start(out=scale_all[:], in_=log_scale.partition_broadcast(P))
        neg_slope = consts.tile([P, 1], F32, name="neg_slope")

        wq_rows = consts.tile([P, F_CHUNKS, D + 2], BF16, name="wq_rows")
        nc.sync.dma_start(
            out=wq_rows[:, :, 0 : D + 1], in_=Wq_last.rearrange("(r p) f -> p r f", p=P)
        )
        nc.sync.dma_start(
            out=load_rows[P - 1 : P, :], in_=load.rearrange("(o b) n -> o (b n)", o=1)
        )
        load_by_tile = load_rows[:].rearrange("q (b i p) -> q b i p", b=B, i=TILES_PER_BATCH)

        load_queries(0)

        ident_f32 = consts.tile([P, P], F32, name="ident_f32")
        make_identity(nc, ident_f32[:])
        ident_bf16 = consts.tile([P, P], BF16, name="ident_bf16")
        make_identity(nc, ident_bf16[:])

        for g in range(PASSES):
            ek = stage.tile([P, PACK, D], F32, name="ek")
            key_exp[(0, g)] = ek
            for cols in HALVES:
                for js in (slice(0, PACK // 2), slice(PACK // 2, PACK)):
                    nc.scalar.activation(
                        out=ek[:, js, cols], in_=key_loads[(0, g)][:, js, cols], func=ACT.Exp
                    )
        quantise_keys(0, "ekv")
        nc.vector.scalar_tensor_tensor(
            out=neg_slope[:], in0=alpha_all[:], scalar=-1.0, in1=scale_all[:],
            op0=ALU.mult, op1=ALU.mult,
        )
        form_exponents(0)
        quantise_keys(0, "ek")

        wq_t = consts.tile([P, F_CHUNKS + 1, D], BF16, name="wq_t")
        for c in range(F_CHUNKS + 1):
            first = min(c * P, D + 1 - P)
            wq_ps = psum_out.tile([P, F_CHUNKS, P], BF16, name="wq_ps", tag="out_bank")
            for r in range(F_CHUNKS):
                nc.tensor.transpose(
                    wq_ps[:, r, :], wq_rows[:, r, first : first + P], ident_bf16[:]
                )
            nc.scalar.copy(out=wq_t[:, c, :], in_=wq_ps[:].rearrange("p r d -> p (r d)"))

        for step in range(FIRST_STEP, LAST_STEP + 1):
            key_load, rest = divmod(step + KEY_LOAD_LEAD, PIECES_PER_PASS)
            if rest == 0 and PASSES <= key_load < B * PASSES:
                load_keys(key_load // PASSES, key_load % PASSES)
            batch, g = divmod(step + VALUE_LEAD, TILES_PER_BATCH)
            if 1 <= batch < B and g < PASSES:
                load_values(batch, g)
            query_load, rest = divmod(step + LOAD_LEAD, LOAD_TILES)
            if rest == 0 and 0 < query_load < TILES // LOAD_TILES:
                load_queries(query_load)

            if is_tile(step + EXP_LEAD) and (step + EXP_LEAD) % 2 == 1:
                copy_node_t(step + EXP_LEAD, nc.vector.tensor_copy)
            if is_tile(step + EXPONENT_LEAD) and step + EXPONENT_LEAD > 0:
                form_exponents(step + EXPONENT_LEAD)
            if is_tile(step):
                quantise_scores(step)
            if is_tile(step - MERGE_LAG) and step - MERGE_LAG != TILES - 2:
                merge_gate_and_num(step - MERGE_LAG)
            if is_tile(step - FINISH_LAG):
                finish(step - FINISH_LAG)
            if step == TILES + 1:
                reciprocal_by_vector(TILES - TILES_PER_BATCH + 1)

            batch, rest = divmod(step, TILES_PER_BATCH)
            if rest == 0 and 1 <= batch < B:
                quantise_keys(batch, "ekv")
                quantise_keys(batch, "ek")
            if step != TILES - 1:
                project_and_transpose(step, step + TRANSPOSE_LEAD)
            if step == TILES - 2:
                project_and_transpose(step + 1, TILES)
            if is_tile(step - NUM_LAG):
                num_ps[step - NUM_LAG] = mix(step - NUM_LAG, "ekv")

            if is_tile(step + EXP_LEAD) and (step + EXP_LEAD) % 2 == 0:
                copy_node_t(step + EXP_LEAD, nc.scalar.copy)
            if is_tile(step + EXP_LEAD):
                exp_scores(step + EXP_LEAD)
            if is_tile(step - NUM_LAG) and step - NUM_LAG < TILES - 1:
                tanh_gate(step - NUM_LAG)
            if PIECES_PER_BATCH <= step + KEY_LEAD < PIECES:
                exp_keys(step + KEY_LEAD)
            if is_tile(step - RECIP_LAG):
                reciprocal_of_den(step - RECIP_LAG)

            batch, rest = divmod(step + 1, TILES_PER_BATCH)
            if rest == 0 and 1 <= batch <= B:
                first = (batch - 1) * TILES_PER_BATCH
                if batch == B:
                    tanh_gate(step)
                    merge_gate_and_num(step - 1)
                for t in range(first, batch * TILES_PER_BATCH):
                    log_of_den(t)
                if batch == B:
                    reciprocal_by_vector(TILES - TILES_PER_BATCH)
